import numpy as np
import ml_dtypes


def mxq(x, axis, fmt="e4m3"):
    dtype, down = {"e4m3": (ml_dtypes.float8_e4m3fn, 7), "e5m2": (ml_dtypes.float8_e5m2, 14)}[fmt]
    v = np.moveaxis(np.asarray(x, np.float32).astype(ml_dtypes.bfloat16).astype(np.float64), axis, -1)
    blocks = v.reshape(v.shape[:-1] + (-1, 32))
    amax = np.abs(blocks).max(-1, keepdims=True)
    byte = np.maximum(np.where(amax > 0, np.frexp(amax)[1] - 1 + 127, 0) - down, 1)
    scale = np.exp2(byte - 127.0)
    codes = (blocks / scale).astype(np.float32).astype(dtype).astype(np.float64)
    return np.moveaxis((codes * scale).reshape(v.shape), -1, axis)


WIDE = False


def mx_kscale(k):
    if not WIDE:
        return np.ones(k)
    levels = np.array([10, -10, 5, -5, 0])
    a = np.random.permutation(np.resize(levels, k // 512 * 4)).reshape(k // 512, 4)
    idx = np.arange(k)
    return np.exp2(a[idx // 512, idx % 128 // 32])


BF16 = ml_dtypes.bfloat16


def bf(x):
    return np.asarray(x, np.float32).astype(BF16)


def f64(x):
    return np.asarray(x).astype(np.float64)


B, S, D, NH, HD, HID = 2, 128, 768, 4, 128, 16384


def setup_inputs():
    t = mx_kscale(HID)
    lengths = np.random.randint(S // 2, S + 1, size=B)
    tail = 0.05 + 0.45 * np.random.random_sample((B, S))
    mask = np.where(np.arange(S)[None, :] < lengths[:, None], 1.0, tail)
    h = np.random.standard_normal((NH, B, S, HD)) + 0.3 * np.random.standard_normal((NH, 1, 1, HD))
    return {"h_heads": bf(h),
            "attention_mask": bf(mask),
            "W1": bf(np.random.standard_normal((NH, HID, HD)) / np.sqrt(HD) * t[None, :, None]),
            "b1": bf(np.random.standard_normal((NH, HID)) * 0.2 * t[None, :]),
            "W2": bf(np.random.standard_normal((NH, HD, HID)) * 2.5 / np.sqrt(HID) / t[None, None, :])}


def reference(h_heads, attention_mask, W1, b1, W2):
    h = f64(h_heads)
    pre = h.reshape(NH, B * S, HD) @ f64(W1).transpose(0, 2, 1) + f64(b1)[:, None, :]
    hid = np.maximum(pre, 0.0)
    a = mxq(hid, 2, "e4m3") @ mxq(f64(W2), 2, "e4m3").transpose(0, 2, 1)
    with np.errstate(divide="ignore"):
        log_mask = np.log(f64(attention_mask))[None, :, :, None]
    a = a.reshape(NH, B, S, HD) + log_mask
    e = np.exp(a - a.max(axis=2, keepdims=True))
    w = e / e.sum(axis=2, keepdims=True)
    v = (h * w).sum(axis=2)
    return v.transpose(1, 0, 2).reshape(B, NH * HD)

@@ -1,0 +1,288 @@
+from contextlib import ExitStack
+
+import concourse.mybir as mybir
+from concourse.masks import make_identity
+
+BF16 = mybir.dt.bfloat16
+F32 = mybir.dt.float32
+U32 = mybir.dt.uint32
+U8 = mybir.dt.uint8
+FP8X4 = mybir.dt.float8_e4m3fn_x4
+ACT = mybir.ActivationFunctionType
+ALU = mybir.AluOpType
+AXIS = mybir.AxisListType
+
+P = 128
+HEADS = 4
+SENTENCES = 2
+TOKENS = 128
+FEAT = 128
+HID = 16384
+NTOK = SENTENCES * TOKENS
+
+PACK = 4
+K_PASS = P * PACK
+CHUNK = P
+
+STEP_PASSES = 2
+STEP_HID = STEP_PASSES * K_PASS
+STEP_CHUNKS = STEP_PASSES * PACK
+STEPS_PER_HEAD = HID // STEP_HID
+STEPS = HEADS * STEPS_PER_HEAD
+
+LOAD_STEPS = 2
+LOAD_HID = LOAD_STEPS * STEP_HID
+LOADS_PER_HEAD = HID // LOAD_HID
+LOADS = HEADS * LOADS_PER_HEAD
+LOADS_AHEAD = 3
+
+FLOPS = 2 * (2 * HEADS * NTOK * FEAT * HID)
+
+
+def tile_multiheadgeneralizedpooling_pa_k_kernel(
+    tc, h_heads, attention_mask, W1, b1, W2, out
+):
+    nc = tc.nc
+    with ExitStack() as ctx:
+        const = ctx.enter_context(tc.tile_pool(name="const", bufs=1))
+        raw = ctx.enter_context(tc.tile_pool(name="raw", bufs=LOADS_AHEAD + 1))
+        work = ctx.enter_context(tc.tile_pool(name="work", bufs=3))
+        codes = ctx.enter_context(tc.tile_pool(name="codes", bufs=4))
+        small = ctx.enter_context(tc.tile_pool(name="small", bufs=2))
+        psum = ctx.enter_context(tc.psum_pool(name="psum", bufs=1))
+
+        def load_weights(load):
+            head, part = divmod(load, LOADS_PER_HEAD)
+            units = slice(part * LOAD_HID, (part + 1) * LOAD_HID)
+            w1_raw = raw.tile([P, LOAD_HID // (2 * P), 2 * FEAT], BF16)
+            nc.sync.dma_start(
+                out=w1_raw[:],
+                in_=W1[head, units, :].rearrange("(c p e) d -> p c (e d)", p=P, e=2),
+            )
+            w2_raw = raw.tile([P, LOAD_HID], BF16)
+            nc.sync.dma_start(out=w2_raw[:], in_=W2[head, :, units])
+            return w1_raw, w2_raw
+
+        h_raw = const.tile([P, HEADS * SENTENCES, FEAT], BF16)
+        nc.sync.dma_start(out=h_raw[:], in_=h_heads.rearrange("i b s d -> s (i b) d"))
+        raw_tiles = {}
+        raw_tiles[0] = load_weights(0)
+        b_raw = const.tile([P, 2, 2 * P], BF16)
+        nc.sync.dma_start(
+            out=b_raw[:],
+            in_=b1.rearrange("i (r c) -> (i r) c", c=2 * P).rearrange("(a r) c -> r a c", a=2),
+        )
+        mask_all = const.tile([P, NTOK], BF16)
+        nc.sync.dma_start(
+            out=mask_all[:], in_=attention_mask.rearrange("b s -> (b s)").partition_broadcast(P)
+        )
+        for load in range(1, LOADS_AHEAD):
+            raw_tiles[load] = load_weights(load)
+
+        ident_bf = const.tile([P, P], BF16)
+        make_identity(nc, ident_bf[:])
+        ident_f32 = const.tile([P, P], F32)
+        make_identity(nc, ident_f32[:])
+
+        log_mask = const.tile([P, NTOK], F32)
+        nc.scalar.activation(out=log_mask[:], in_=mask_all[:], func=ACT.Ln)
+
+        h_bank = psum.tile([P, STEP_CHUNKS, P], BF16, tag="w1_bank", bufs=2)
+        for ib in range(HEADS * SENTENCES):
+            nc.tensor.transpose(h_bank[:, ib, :], h_raw[:, ib, :], ident_bf[:])
+        hT_bf = const.tile([P, HEADS * NTOK], BF16)
+        nc.vector.tensor_copy(out=hT_bf[:], in_=h_bank[:].rearrange("p c s -> p (c s)"))
+        hT_f32 = const.tile([P, HEADS * NTOK], F32)
+        nc.scalar.copy(out=hT_f32[:], in_=hT_bf[:])
+
+        b_bank = psum.tile([P, 2 * STEP_PASSES, P], F32, tag="w2_bank", bufs=1)
+        b_words = b_raw[:].bitcast(F32)
+        for a in range(2):
+            nc.tensor.transpose(b_bank[:, a, :], b_words[:, a, :], ident_f32[:])
+        bias = const.tile([P, HEADS * HID // CHUNK], F32)
+        nc.scalar.copy(
+            out=bias[:].rearrange("p (a c) -> p a c", a=2), in_=b_bank[:].bitcast(BF16)[:, 0:2, :]
+        )
+
+        pooled = const.tile([P, P], F32)
+        nc.vector.memset(pooled[:], 0.0)
+
+        w1T_tiles = {}
+        w2_grouped_tiles = {}
+        w2_mx = {}
+        plane_tiles = {}
+        hid_grouped_tiles = {}
+        hid_mx = {}
+        score_banks = {}
+
+        def transpose_weights(step):
+            w1_raw, w2_raw = raw_tiles[step // LOAD_STEPS]
+            local = step % LOAD_STEPS
+            w1_bank = psum.tile([P, STEP_CHUNKS, P], BF16, tag="w1_bank", bufs=2)
+            for c in range(STEP_CHUNKS):
+                pair, e = divmod(local * STEP_CHUNKS + c, 2)
+                nc.tensor.transpose(
+                    w1_bank[:, c, :], w1_raw[:, pair, e * FEAT : (e + 1) * FEAT], ident_bf[:]
+                )
+            w2_words = w2_raw[:].bitcast(F32)
+            w2_bank = psum.tile([P, 2 * STEP_PASSES, P], F32, tag="w2_bank", bufs=1)
+            for gu in range(2 * STEP_PASSES):
+                first = (local * 2 * STEP_PASSES + gu) * P
+                nc.tensor.transpose(w2_bank[:, gu, :], w2_words[:, first : first + P], ident_f32[:])
+
+            w1T = work.tile([P, STEP_CHUNKS, CHUNK], BF16)
+            if step % 2 == 0:
+                nc.vector.tensor_copy(out=w1T[:], in_=w1_bank[:])
+            else:
+                nc.scalar.copy(out=w1T[:], in_=w1_bank[:])
+            w1T_tiles[step] = w1T
+
+            w2_grouped = work.tile([P, STEP_PASSES * FEAT * PACK], BF16, align_bytes=64)
+            nc.vector.tensor_copy(
+                out=w2_grouped[:].bitcast(F32).rearrange("p (g d u) -> p g d u", d=FEAT, u=2),
+                in_=w2_bank[:].rearrange("p (g u) d -> p g d u", u=2),
+            )
+            w2_grouped_tiles[step] = w2_grouped
+
+        def quantise_w2(step):
+            w2_codes = codes.tile([P, STEP_PASSES * FEAT], U32, align_bytes=64)
+            w2_scales = codes.tile([P, STEP_PASSES * FEAT], U8, align_bytes=64)
+            nc.vector.quantize_mx(
+                out=w2_codes[:].bitcast(FP8X4), scales=w2_scales[:], in_=w2_grouped_tiles[step][:]
+            )
+            w2_mx[step] = (w2_codes, w2_scales)
+
+        def hidden_layer(step):
+            head = step // STEPS_PER_HEAD
+            w1T = w1T_tiles[step]
+            planes = work.tile([P, PACK, STEP_PASSES * NTOK], BF16)
+            for pair in range(STEP_CHUNKS // 2):
+                hid_bank = psum.tile([P, 2, NTOK], F32, tag="hid_bank", bufs=4)
+                for half in range(2):
+                    nc.tensor.matmul(
+                        hid_bank[:, half, :],
+                        lhsT=w1T[:, 2 * pair + half, :],
+                        rhs=hT_bf[:, head * NTOK : (head + 1) * NTOK],
+                        start=True,
+                        stop=True,
+                    )
+                for half in range(2):
+                    chunk = 2 * pair + half
+                    g, t = divmod(chunk, PACK)
+                    column = step * STEP_CHUNKS + chunk
+                    nc.scalar.activation(
+                        out=planes[:, t, g * NTOK : (g + 1) * NTOK],
+                        in_=hid_bank[:, half, :],
+                        func=ACT.Relu,
+                        bias=bias[:, column : column + 1],
+                        scale=1.0,
+                    )
+            plane_tiles[step] = planes
+
+        def group_hidden(step):
+            planes = plane_tiles[step]
+            hid_grouped = work.tile([P, STEP_PASSES * NTOK * PACK], BF16, align_bytes=64)
+            nc.vector.tensor_copy(
+                out=hid_grouped[:].rearrange("p (c i t) -> p c t i", i=4, t=PACK),
+                in_=planes[:].rearrange("p t (c i) -> p c t i", i=4),
+            )
+            hid_grouped_tiles[step] = hid_grouped
+
+        def quantise_hidden(step):
+            hid_codes = codes.tile([P, STEP_PASSES * NTOK], U32, align_bytes=64)
+            hid_scales = codes.tile([P, STEP_PASSES * NTOK], U8, align_bytes=64)
+            nc.vector.quantize_mx(
+                out=hid_codes[:].bitcast(FP8X4),
+                scales=hid_scales[:],
+                in_=hid_grouped_tiles[step][:],
+            )
+            hid_mx[step] = (hid_codes, hid_scales)
+
+        def second_layer(step):
+            head, part = divmod(step, STEPS_PER_HEAD)
+            if part == 0:
+                scores = psum.tile([P, NTOK], F32, tag="scores", bufs=1)
+                score_banks[head] = scores
+            scores = score_banks[head]
+            w2_codes, w2_scales = w2_mx[step]
+            hid_codes, hid_scales = hid_mx[step]
+            for g in range(STEP_PASSES):
+                feats = slice(g * FEAT, (g + 1) * FEAT)
+                toks = slice(g * NTOK, (g + 1) * NTOK)
+                nc.tensor.matmul_mx(
+                    out=scores[:],
+                    lhsT=w2_codes[:, feats].bitcast(FP8X4),
+                    lhsT_scale=w2_scales[:, feats],
+                    rhs=hid_codes[:, toks].bitcast(FP8X4),
+                    rhs_scale=hid_scales[:, toks],
+                    start=(part == 0 and g == 0),
+                    stop=(part == STEPS_PER_HEAD - 1 and g == STEP_PASSES - 1),
+                )
+
+        def pool_head(head):
+            a = small.tile([P, SENTENCES, TOKENS], F32)
+            nc.vector.tensor_tensor(
+                out=a[:].rearrange("p b s -> p (b s)"),
+                in0=score_banks[head][:],
+                in1=log_mask[:],
+                op=ALU.add,
+            )
+            a_max = small.tile([P, SENTENCES], F32)
+            nc.vector.tensor_reduce(out=a_max[:], in_=a[:], axis=AXIS.X, op=ALU.max)
+            neg_max = small.tile([P, SENTENCES], F32)
+            nc.vector.tensor_scalar_mul(out=neg_max[:], in0=a_max[:], scalar1=-1.0)
+            e = small.tile([P, SENTENCES, TOKENS], F32)
+            e_sum = small.tile([P, SENTENCES], F32)
+            for b in range(SENTENCES):
+                nc.scalar.activation(
+                    out=e[:, b, :],
+                    in_=a[:, b, :],
+                    func=ACT.Exp,
+                    bias=neg_max[:, b : b + 1],
+                    scale=1.0,
+                    accum_out=e_sum[:, b : b + 1],
+                )
+            he = small.tile([P, SENTENCES, TOKENS], F32)
+            nc.vector.tensor_tensor(
+                out=he[:].rearrange("p b s -> p (b s)"),
+                in0=e[:].rearrange("p b s -> p (b s)"),
+                in1=hT_f32[:, head * NTOK : (head + 1) * NTOK],
+                op=ALU.mult,
+            )
+            he_sum = small.tile([P, SENTENCES], F32)
+            nc.vector.tensor_reduce(out=he_sum[:], in_=he[:], axis=AXIS.X, op=ALU.add)
+            inv_sum = small.tile([P, SENTENCES], F32)
+            nc.vector.reciprocal(out=inv_sum[:], in_=e_sum[:])
+            nc.vector.tensor_tensor(
+                out=pooled[:, 0 : SENTENCES * HEADS].rearrange("p (b i) -> p b i", i=HEADS)[:, :, head],
+                in0=he_sum[:],
+                in1=inv_sum[:],
+                op=ALU.mult,
+            )
+
+        for r in range(-1, STEPS + 2):
+            if 0 <= r - 2:
+                second_layer(r - 2)
+                if (r - 2) % STEPS_PER_HEAD == STEPS_PER_HEAD - 1:
+                    pool_head((r - 2) // STEPS_PER_HEAD)
+            if r + 1 < STEPS:
+                if (r + 1) % LOAD_STEPS == 0 and (r + 1) // LOAD_STEPS + LOADS_AHEAD < LOADS:
+                    load = (r + 1) // LOAD_STEPS + LOADS_AHEAD
+                    raw_tiles[load] = load_weights(load)
+                transpose_weights(r + 1)
+            if 0 <= r < STEPS:
+                hidden_layer(r)
+            if 0 <= r - 1 < STEPS:
+                group_hidden(r - 1)
+            if r + 1 < STEPS:
+                quantise_w2(r + 1)
+            if 0 <= r - 1 < STEPS:
+                quantise_hidden(r - 1)
+
+        out_bank = psum.tile([P, 2 * STEP_PASSES, P], F32, tag="w2_bank", bufs=1)
+        nc.tensor.transpose(out_bank[:, 0, :], pooled[:], ident_f32[:])
+        out_rows = small.tile([P, FEAT], F32)
+        nc.vector.tensor_copy(out=out_rows[:], in_=out_bank[:, 0, :])
+        nc.sync.dma_start(
+            out=out.rearrange("b (i d) -> (b i) d", d=FEAT), in_=out_rows[0 : SENTENCES * HEADS, :]
+        )

@@ -47,9 +47,10 @@ def tile_multiheadgeneralizedpooling_pa_k_kernel(
         const = ctx.enter_context(tc.tile_pool(name="const", bufs=1))
         raw = ctx.enter_context(tc.tile_pool(name="raw", bufs=LOADS_AHEAD + 1))
         work = ctx.enter_context(tc.tile_pool(name="work", bufs=3))
-        codes = ctx.enter_context(tc.tile_pool(name="codes", bufs=4))
+        codes = ctx.enter_context(tc.tile_pool(name="codes", bufs=6))
         small = ctx.enter_context(tc.tile_pool(name="small", bufs=2))
         psum = ctx.enter_context(tc.psum_pool(name="psum", bufs=1))
+        ctx.enter_context(tc.manual_schedule())
 
         def load_weights(load):
             head, part = divmod(load, LOADS_PER_HEAD)
@@ -63,20 +64,19 @@ def tile_multiheadgeneralizedpooling_pa_k_kernel(
             nc.sync.dma_start(out=w2_raw[:], in_=W2[head, :, units])
             return w1_raw, w2_raw
 
-        h_raw = const.tile([P, HEADS * SENTENCES, FEAT], BF16)
-        nc.sync.dma_start(out=h_raw[:], in_=h_heads.rearrange("i b s d -> s (i b) d"))
-        raw_tiles = {}
-        raw_tiles[0] = load_weights(0)
+        mask_all = const.tile([P, NTOK], BF16)
+        nc.scalar.dma_start(
+            out=mask_all[:], in_=attention_mask.rearrange("b s -> (b s)").partition_broadcast(P)
+        )
         b_raw = const.tile([P, 2, 2 * P], BF16)
-        nc.sync.dma_start(
+        nc.scalar.dma_start(
             out=b_raw[:],
             in_=b1.rearrange("i (r c) -> (i r) c", c=2 * P).rearrange("(a r) c -> r a c", a=2),
         )
-        mask_all = const.tile([P, NTOK], BF16)
-        nc.sync.dma_start(
-            out=mask_all[:], in_=attention_mask.rearrange("b s -> (b s)").partition_broadcast(P)
-        )
-        for load in range(1, LOADS_AHEAD):
+        h_raw = const.tile([P, HEADS * SENTENCES, FEAT], BF16)
+        nc.sync.dma_start(out=h_raw[:], in_=h_heads.rearrange("i b s d -> s (i b) d"))
+        raw_tiles = {}
+        for load in range(LOADS_AHEAD):
             raw_tiles[load] = load_weights(load)
 
         ident_bf = const.tile([P, P], BF16)
@@ -107,6 +107,7 @@ def tile_multiheadgeneralizedpooling_pa_k_kernel(
         pooled = const.tile([P, P], F32)
         nc.vector.memset(pooled[:], 0.0)
 
+        weight_banks = {}
         w1T_tiles = {}
         w2_grouped_tiles = {}
         w2_mx = {}
@@ -129,9 +130,12 @@ def tile_multiheadgeneralizedpooling_pa_k_kernel(
             for gu in range(2 * STEP_PASSES):
                 first = (local * 2 * STEP_PASSES + gu) * P
                 nc.tensor.transpose(w2_bank[:, gu, :], w2_words[:, first : first + P], ident_f32[:])
+            weight_banks[step] = (w1_bank, w2_bank)
 
+        def empty_weight_banks(step):
+            w1_bank, w2_bank = weight_banks[step]
             w1T = work.tile([P, STEP_CHUNKS, CHUNK], BF16)
-            if step % 2 == 0:
+            if step % 3 == 0:
                 nc.vector.tensor_copy(out=w1T[:], in_=w1_bank[:])
             else:
                 nc.scalar.copy(out=w1T[:], in_=w1_bank[:])
@@ -260,23 +264,28 @@ def tile_multiheadgeneralizedpooling_pa_k_kernel(
                 op=ALU.mult,
             )
 
-        for r in range(-1, STEPS + 2):
-            if 0 <= r - 2:
-                second_layer(r - 2)
-                if (r - 2) % STEPS_PER_HEAD == STEPS_PER_HEAD - 1:
-                    pool_head((r - 2) // STEPS_PER_HEAD)
-            if r + 1 < STEPS:
-                if (r + 1) % LOAD_STEPS == 0 and (r + 1) // LOAD_STEPS + LOADS_AHEAD < LOADS:
-                    load = (r + 1) // LOAD_STEPS + LOADS_AHEAD
+        def is_step(step):
+            return 0 <= step < STEPS
+
+        for r in range(-1, STEPS + 3):
+            if is_step(r + 1):
+                load = (r + 1) // LOAD_STEPS + LOADS_AHEAD
+                if (r + 1) % LOAD_STEPS == 0 and load < LOADS:
                     raw_tiles[load] = load_weights(load)
                 transpose_weights(r + 1)
-            if 0 <= r < STEPS:
+            if is_step(r - 3):
+                second_layer(r - 3)
+                if (r - 3) % STEPS_PER_HEAD == STEPS_PER_HEAD - 1:
+                    pool_head((r - 3) // STEPS_PER_HEAD)
+            if is_step(r + 1):
+                empty_weight_banks(r + 1)
+            if is_step(r):
                 hidden_layer(r)
-            if 0 <= r - 1 < STEPS:
+            if is_step(r - 1):
                 group_hidden(r - 1)
-            if r + 1 < STEPS:
+            if is_step(r + 1):
                 quantise_w2(r + 1)
-            if 0 <= r - 1 < STEPS:
+            if is_step(r - 1):
                 quantise_hidden(r - 1)
 
         out_bank = psum.tile([P, 2 * STEP_PASSES, P], F32, tag="w2_bank", bufs=1)

@@ -115,6 +115,8 @@ def tile_multiheadgeneralizedpooling_pa_k_kernel(
         hid_grouped_tiles = {}
         hid_mx = {}
         score_banks = {}
+        softmax_tiles = {}
+        exp_tiles = {}
 
         def transpose_weights(step):
             w1_raw, w2_raw = raw_tiles[step // LOAD_STEPS]
@@ -134,19 +136,17 @@ def tile_multiheadgeneralizedpooling_pa_k_kernel(
 
         def empty_weight_banks(step):
             w1_bank, w2_bank = weight_banks[step]
-            w1T = work.tile([P, STEP_CHUNKS, CHUNK], BF16)
-            if step % 3 == 0:
-                nc.vector.tensor_copy(out=w1T[:], in_=w1_bank[:])
-            else:
-                nc.scalar.copy(out=w1T[:], in_=w1_bank[:])
-            w1T_tiles[step] = w1T
-
             w2_grouped = work.tile([P, STEP_PASSES * FEAT * PACK], BF16, align_bytes=64)
-            nc.vector.tensor_copy(
-                out=w2_grouped[:].bitcast(F32).rearrange("p (g d u) -> p g d u", d=FEAT, u=2),
-                in_=w2_bank[:].rearrange("p (g u) d -> p g d u", u=2),
-            )
+            w2_pairs = w2_grouped[:].bitcast(F32).rearrange("p (g d u) -> p g d u", d=FEAT, u=2)
+            w2_planes = w2_bank[:].rearrange("p (g u) d -> p g d u", u=2)
+            if step % 4 == 0:
+                nc.vector.tensor_copy(out=w2_pairs, in_=w2_planes)
+            else:
+                nc.scalar.copy(out=w2_pairs, in_=w2_planes)
             w2_grouped_tiles[step] = w2_grouped
+            w1T = work.tile([P, STEP_CHUNKS, CHUNK], BF16)
+            nc.vector.tensor_copy(out=w1T[:], in_=w1_bank[:])
+            w1T_tiles[step] = w1T
 
         def quantise_w2(step):
             w2_codes = codes.tile([P, STEP_PASSES * FEAT], U32, align_bytes=64)
@@ -223,7 +223,7 @@ def tile_multiheadgeneralizedpooling_pa_k_kernel(
                     stop=(part == STEPS_PER_HEAD - 1 and g == STEP_PASSES - 1),
                 )
 
-        def pool_head(head):
+        def softmax_shift(head):
             a = small.tile([P, SENTENCES, TOKENS], F32)
             nc.vector.tensor_tensor(
                 out=a[:].rearrange("p b s -> p (b s)"),
@@ -235,6 +235,10 @@ def tile_multiheadgeneralizedpooling_pa_k_kernel(
             nc.vector.tensor_reduce(out=a_max[:], in_=a[:], axis=AXIS.X, op=ALU.max)
             neg_max = small.tile([P, SENTENCES], F32)
             nc.vector.tensor_scalar_mul(out=neg_max[:], in0=a_max[:], scalar1=-1.0)
+            softmax_tiles[head] = (a, neg_max)
+
+        def softmax_exp(head):
+            a, neg_max = softmax_tiles[head]
             e = small.tile([P, SENTENCES, TOKENS], F32)
             e_sum = small.tile([P, SENTENCES], F32)
             for b in range(SENTENCES):
@@ -246,6 +250,10 @@ def tile_multiheadgeneralizedpooling_pa_k_kernel(
                     scale=1.0,
                     accum_out=e_sum[:, b : b + 1],
                 )
+            exp_tiles[head] = (e, e_sum)
+
+        def weighted_sum(head):
+            e, e_sum = exp_tiles[head]
             he = small.tile([P, SENTENCES, TOKENS], F32)
             nc.vector.tensor_tensor(
                 out=he[:].rearrange("p b s -> p (b s)"),
@@ -267,7 +275,10 @@ def tile_multiheadgeneralizedpooling_pa_k_kernel(
         def is_step(step):
             return 0 <= step < STEPS
 
-        for r in range(-1, STEPS + 3):
+        def ends_a_head(step):
+            return is_step(step) and step % STEPS_PER_HEAD == STEPS_PER_HEAD - 1
+
+        for r in range(-1, STEPS + 4):
             if is_step(r + 1):
                 load = (r + 1) // LOAD_STEPS + LOADS_AHEAD
                 if (r + 1) % LOAD_STEPS == 0 and load < LOADS:
@@ -275,18 +286,22 @@ def tile_multiheadgeneralizedpooling_pa_k_kernel(
                 transpose_weights(r + 1)
             if is_step(r - 3):
                 second_layer(r - 3)
-                if (r - 3) % STEPS_PER_HEAD == STEPS_PER_HEAD - 1:
-                    pool_head((r - 3) // STEPS_PER_HEAD)
+            if ends_a_head(r - 3):
+                softmax_shift((r - 3) // STEPS_PER_HEAD)
             if is_step(r + 1):
                 empty_weight_banks(r + 1)
             if is_step(r):
                 hidden_layer(r)
+            if ends_a_head(r - 3):
+                softmax_exp((r - 3) // STEPS_PER_HEAD)
             if is_step(r - 1):
                 group_hidden(r - 1)
             if is_step(r + 1):
                 quantise_w2(r + 1)
             if is_step(r - 1):
                 quantise_hidden(r - 1)
+            if ends_a_head(r - 4):
+                weighted_sum((r - 4) // STEPS_PER_HEAD)
 
         out_bank = psum.tile([P, 2 * STEP_PASSES, P], F32, tag="w2_bank", bufs=1)
         nc.tensor.transpose(out_bank[:, 0, :], pooled[:], ident_f32[:])

from contextlib import ExitStack

import concourse.mybir as mybir
from concourse.masks import make_identity

BF16 = mybir.dt.bfloat16
F32 = mybir.dt.float32
U32 = mybir.dt.uint32
U8 = mybir.dt.uint8
FP8X4 = mybir.dt.float8_e4m3fn_x4
ACT = mybir.ActivationFunctionType
ALU = mybir.AluOpType
AXIS = mybir.AxisListType

P = 128
HEADS = 4
SENTENCES = 2
TOKENS = 128
FEAT = 128
HID = 16384
NTOK = SENTENCES * TOKENS

PACK = 4
K_PASS = P * PACK
CHUNK = P

STEP_PASSES = 2
STEP_HID = STEP_PASSES * K_PASS
STEP_CHUNKS = STEP_PASSES * PACK
STEPS_PER_HEAD = HID // STEP_HID
STEPS = HEADS * STEPS_PER_HEAD

LOAD_STEPS = 2
LOAD_HID = LOAD_STEPS * STEP_HID
LOADS_PER_HEAD = HID // LOAD_HID
LOADS = HEADS * LOADS_PER_HEAD
LOADS_AHEAD = 3

FLOPS = 2 * (2 * HEADS * NTOK * FEAT * HID)


def tile_multiheadgeneralizedpooling_pa_k_kernel(
    tc, h_heads, attention_mask, W1, b1, W2, out
):
    nc = tc.nc
    with ExitStack() as ctx:
        const = ctx.enter_context(tc.tile_pool(name="const", bufs=1))
        raw = ctx.enter_context(tc.tile_pool(name="raw", bufs=LOADS_AHEAD + 1))
        work = ctx.enter_context(tc.tile_pool(name="work", bufs=3))
        codes = ctx.enter_context(tc.tile_pool(name="codes", bufs=6))
        small = ctx.enter_context(tc.tile_pool(name="small", bufs=2))
        psum = ctx.enter_context(tc.psum_pool(name="psum", bufs=1))
        ctx.enter_context(tc.manual_schedule())

        def load_weights(load):
            head, part = divmod(load, LOADS_PER_HEAD)
            units = slice(part * LOAD_HID, (part + 1) * LOAD_HID)
            w1_raw = raw.tile([P, LOAD_HID // (2 * P), 2 * FEAT], BF16)
            nc.sync.dma_start(
                out=w1_raw[:],
                in_=W1[head, units, :].rearrange("(c p e) d -> p c (e d)", p=P, e=2),
            )
            w2_raw = raw.tile([P, LOAD_HID], BF16)
            nc.sync.dma_start(out=w2_raw[:], in_=W2[head, :, units])
            return w1_raw, w2_raw

        mask_all = const.tile([P, NTOK], BF16)
        nc.scalar.dma_start(
            out=mask_all[:], in_=attention_mask.rearrange("b s -> (b s)").partition_broadcast(P)
        )
        b_raw = const.tile([P, 2, 2 * P], BF16)
        nc.scalar.dma_start(
            out=b_raw[:],
            in_=b1.rearrange("i (r c) -> (i r) c", c=2 * P).rearrange("(a r) c -> r a c", a=2),
        )
        h_raw = const.tile([P, HEADS * SENTENCES, FEAT], BF16)
        nc.sync.dma_start(out=h_raw[:], in_=h_heads.rearrange("i b s d -> s (i b) d"))
        raw_tiles = {}
        for load in range(LOADS_AHEAD):
            raw_tiles[load] = load_weights(load)

        ident_bf = const.tile([P, P], BF16)
        make_identity(nc, ident_bf[:])
        ident_f32 = const.tile([P, P], F32)
        make_identity(nc, ident_f32[:])

        log_mask = const.tile([P, NTOK], F32)
        nc.scalar.activation(out=log_mask[:], in_=mask_all[:], func=ACT.Ln)

        h_bank = psum.tile([P, STEP_CHUNKS, P], BF16, tag="w1_bank", bufs=2)
        for ib in range(HEADS * SENTENCES):
            nc.tensor.transpose(h_bank[:, ib, :], h_raw[:, ib, :], ident_bf[:])
        hT_bf = const.tile([P, HEADS * NTOK], BF16)
        nc.vector.tensor_copy(out=hT_bf[:], in_=h_bank[:].rearrange("p c s -> p (c s)"))
        hT_f32 = const.tile([P, HEADS * NTOK], F32)
        nc.scalar.copy(out=hT_f32[:], in_=hT_bf[:])

        b_bank = psum.tile([P, 2 * STEP_PASSES, P], F32, tag="w2_bank", bufs=1)
        b_words = b_raw[:].bitcast(F32)
        for a in range(2):
            nc.tensor.transpose(b_bank[:, a, :], b_words[:, a, :], ident_f32[:])
        bias = const.tile([P, HEADS * HID // CHUNK], F32)
        nc.scalar.copy(
            out=bias[:].rearrange("p (a c) -> p a c", a=2), in_=b_bank[:].bitcast(BF16)[:, 0:2, :]
        )

        pooled = const.tile([P, P], F32)
        nc.vector.memset(pooled[:], 0.0)

        weight_banks = {}
        w1T_tiles = {}
        w2_grouped_tiles = {}
        w2_mx = {}
        plane_tiles = {}
        hid_grouped_tiles = {}
        hid_mx = {}
        score_banks = {}
        softmax_tiles = {}
        exp_tiles = {}

        def transpose_weights(step):
            w1_raw, w2_raw = raw_tiles[step // LOAD_STEPS]
            local = step % LOAD_STEPS
            w1_bank = psum.tile([P, STEP_CHUNKS, P], BF16, tag="w1_bank", bufs=2)
            for c in range(STEP_CHUNKS):
                pair, e = divmod(local * STEP_CHUNKS + c, 2)
                nc.tensor.transpose(
                    w1_bank[:, c, :], w1_raw[:, pair, e * FEAT : (e + 1) * FEAT], ident_bf[:]
                )
            w2_words = w2_raw[:].bitcast(F32)
            w2_bank = psum.tile([P, 2 * STEP_PASSES, P], F32, tag="w2_bank", bufs=1)
            for gu in range(2 * STEP_PASSES):
                first = (local * 2 * STEP_PASSES + gu) * P
                nc.tensor.transpose(w2_bank[:, gu, :], w2_words[:, first : first + P], ident_f32[:])
            weight_banks[step] = (w1_bank, w2_bank)

        def empty_weight_banks(step):
            w1_bank, w2_bank = weight_banks[step]
            w2_grouped = work.tile([P, STEP_PASSES * FEAT * PACK], BF16, align_bytes=64)
            w2_pairs = w2_grouped[:].bitcast(F32).rearrange("p (g d u) -> p g d u", d=FEAT, u=2)
            w2_planes = w2_bank[:].rearrange("p (g u) d -> p g d u", u=2)
            if step % 4 == 0:
                nc.vector.tensor_copy(out=w2_pairs, in_=w2_planes)
            else:
                nc.scalar.copy(out=w2_pairs, in_=w2_planes)
            w2_grouped_tiles[step] = w2_grouped
            w1T = work.tile([P, STEP_CHUNKS, CHUNK], BF16)
            nc.vector.tensor_copy(out=w1T[:], in_=w1_bank[:])
            w1T_tiles[step] = w1T

        def quantise_w2(step):
            w2_codes = codes.tile([P, STEP_PASSES * FEAT], U32, align_bytes=64)
            w2_scales = codes.tile([P, STEP_PASSES * FEAT], U8, align_bytes=64)
            nc.vector.quantize_mx(
                out=w2_codes[:].bitcast(FP8X4), scales=w2_scales[:], in_=w2_grouped_tiles[step][:]
            )
            w2_mx[step] = (w2_codes, w2_scales)

        def hidden_layer(step):
            head = step // STEPS_PER_HEAD
            w1T = w1T_tiles[step]
            planes = work.tile([P, PACK, STEP_PASSES * NTOK], BF16)
            for pair in range(STEP_CHUNKS // 2):
                hid_bank = psum.tile([P, 2, NTOK], F32, tag="hid_bank", bufs=4)
                for half in range(2):
                    nc.tensor.matmul(
                        hid_bank[:, half, :],
                        lhsT=w1T[:, 2 * pair + half, :],
                        rhs=hT_bf[:, head * NTOK : (head + 1) * NTOK],
                        start=True,
                        stop=True,
                    )
                for half in range(2):
                    chunk = 2 * pair + half
                    g, t = divmod(chunk, PACK)
                    column = step * STEP_CHUNKS + chunk
                    nc.scalar.activation(
                        out=planes[:, t, g * NTOK : (g + 1) * NTOK],
                        in_=hid_bank[:, half, :],
                        func=ACT.Relu,
                        bias=bias[:, column : column + 1],
                        scale=1.0,
                    )
            plane_tiles[step] = planes

        def group_hidden(step):
            planes = plane_tiles[step]
            hid_grouped = work.tile([P, STEP_PASSES * NTOK * PACK], BF16, align_bytes=64)
            nc.vector.tensor_copy(
                out=hid_grouped[:].rearrange("p (c i t) -> p c t i", i=4, t=PACK),
                in_=planes[:].rearrange("p t (c i) -> p c t i", i=4),
            )
            hid_grouped_tiles[step] = hid_grouped

        def quantise_hidden(step):
            hid_codes = codes.tile([P, STEP_PASSES * NTOK], U32, align_bytes=64)
            hid_scales = codes.tile([P, STEP_PASSES * NTOK], U8, align_bytes=64)
            nc.vector.quantize_mx(
                out=hid_codes[:].bitcast(FP8X4),
                scales=hid_scales[:],
                in_=hid_grouped_tiles[step][:],
            )
            hid_mx[step] = (hid_codes, hid_scales)

        def second_layer(step):
            head, part = divmod(step, STEPS_PER_HEAD)
            if part == 0:
                scores = psum.tile([P, NTOK], F32, tag="scores", bufs=1)
                score_banks[head] = scores
            scores = score_banks[head]
            w2_codes, w2_scales = w2_mx[step]
            hid_codes, hid_scales = hid_mx[step]
            for g in range(STEP_PASSES):
                feats = slice(g * FEAT, (g + 1) * FEAT)
                toks = slice(g * NTOK, (g + 1) * NTOK)
                nc.tensor.matmul_mx(
                    out=scores[:],
                    lhsT=w2_codes[:, feats].bitcast(FP8X4),
                    lhsT_scale=w2_scales[:, feats],
                    rhs=hid_codes[:, toks].bitcast(FP8X4),
                    rhs_scale=hid_scales[:, toks],
                    start=(part == 0 and g == 0),
                    stop=(part == STEPS_PER_HEAD - 1 and g == STEP_PASSES - 1),
                )

        def softmax_shift(head):
            a = small.tile([P, SENTENCES, TOKENS], F32)
            nc.vector.tensor_tensor(
                out=a[:].rearrange("p b s -> p (b s)"),
                in0=score_banks[head][:],
                in1=log_mask[:],
                op=ALU.add,
            )
            a_max = small.tile([P, SENTENCES], F32)
            nc.vector.tensor_reduce(out=a_max[:], in_=a[:], axis=AXIS.X, op=ALU.max)
            neg_max = small.tile([P, SENTENCES], F32)
            nc.vector.tensor_scalar_mul(out=neg_max[:], in0=a_max[:], scalar1=-1.0)
            softmax_tiles[head] = (a, neg_max)

        def softmax_exp(head):
            a, neg_max = softmax_tiles[head]
            e = small.tile([P, SENTENCES, TOKENS], F32)
            e_sum = small.tile([P, SENTENCES], F32)
            for b in range(SENTENCES):
                nc.scalar.activation(
                    out=e[:, b, :],
                    in_=a[:, b, :],
                    func=ACT.Exp,
                    bias=neg_max[:, b : b + 1],
                    scale=1.0,
                    accum_out=e_sum[:, b : b + 1],
                )
            exp_tiles[head] = (e, e_sum)

        def weighted_sum(head):
            e, e_sum = exp_tiles[head]
            he = small.tile([P, SENTENCES, TOKENS], F32)
            nc.vector.tensor_tensor(
                out=he[:].rearrange("p b s -> p (b s)"),
                in0=e[:].rearrange("p b s -> p (b s)"),
                in1=hT_f32[:, head * NTOK : (head + 1) * NTOK],
                op=ALU.mult,
            )
            he_sum = small.tile([P, SENTENCES], F32)
            nc.vector.tensor_reduce(out=he_sum[:], in_=he[:], axis=AXIS.X, op=ALU.add)
            inv_sum = small.tile([P, SENTENCES], F32)
            nc.vector.reciprocal(out=inv_sum[:], in_=e_sum[:])
            nc.vector.tensor_tensor(
                out=pooled[:, 0 : SENTENCES * HEADS].rearrange("p (b i) -> p b i", i=HEADS)[:, :, head],
                in0=he_sum[:],
                in1=inv_sum[:],
                op=ALU.mult,
            )

        def is_step(step):
            return 0 <= step < STEPS

        def ends_a_head(step):
            return is_step(step) and step % STEPS_PER_HEAD == STEPS_PER_HEAD - 1

        for r in range(-1, STEPS + 4):
            if is_step(r + 1):
                load = (r + 1) // LOAD_STEPS + LOADS_AHEAD
                if (r + 1) % LOAD_STEPS == 0 and load < LOADS:
                    raw_tiles[load] = load_weights(load)
                transpose_weights(r + 1)
            if is_step(r - 3):
                second_layer(r - 3)
            if ends_a_head(r - 3):
                softmax_shift((r - 3) // STEPS_PER_HEAD)
            if is_step(r + 1):
                empty_weight_banks(r + 1)
            if is_step(r):
                hidden_layer(r)
            if ends_a_head(r - 3):
                softmax_exp((r - 3) // STEPS_PER_HEAD)
            if is_step(r - 1):
                group_hidden(r - 1)
            if is_step(r + 1):
                quantise_w2(r + 1)
            if is_step(r - 1):
                quantise_hidden(r - 1)
            if ends_a_head(r - 4):
                weighted_sum((r - 4) // STEPS_PER_HEAD)

        out_bank = psum.tile([P, 2 * STEP_PASSES, P], F32, tag="w2_bank", bufs=1)
        nc.tensor.transpose(out_bank[:, 0, :], pooled[:], ident_f32[:])
        out_rows = small.tile([P, FEAT], F32)
        nc.vector.tensor_copy(out=out_rows[:], in_=out_bank[:, 0, :])
        nc.sync.dma_start(
            out=out.rearrange("b (i d) -> (b i) d", d=FEAT), in_=out_rows[0 : SENTENCES * HEADS, :]
        )
